import numpy as np
import ml_dtypes


def mxq(x, axis, fmt="e4m3"):
    dtype, down = {"e4m3": (ml_dtypes.float8_e4m3fn, 7), "e5m2": (ml_dtypes.float8_e5m2, 14)}[fmt]
    v = np.moveaxis(np.asarray(x, np.float32).astype(ml_dtypes.bfloat16).astype(np.float64), axis, -1)
    blocks = v.reshape(v.shape[:-1] + (-1, 32))
    amax = np.abs(blocks).max(-1, keepdims=True)
    byte = np.maximum(np.where(amax > 0, np.frexp(amax)[1] - 1 + 127, 0) - down, 1)
    scale = np.exp2(byte - 127.0)
    codes = (blocks / scale).astype(np.float32).astype(dtype).astype(np.float64)
    return np.moveaxis((codes * scale).reshape(v.shape), -1, axis)


WIDE = False


def mx_kscale(k):
    if not WIDE:
        return np.ones(k)
    levels = np.array([20, -20, 10, -10, 0])
    a = np.random.permutation(np.resize(levels, k // 512 * 4)).reshape(k // 512, 4)
    idx = np.arange(k)
    return np.exp2(a[idx // 512, idx % 128 // 32])


BF16 = ml_dtypes.bfloat16


def bf(x):
    return np.asarray(x, np.float32).astype(BF16)


def f64(x):
    return np.asarray(x).astype(np.float64)


B, S, A, O, H, L = 512, 1024, 128, 1920, 1024, 384
G = L + A


def sigmoid(v):
    return 1.0 / (1.0 + np.exp(-v))


def cell(sample, prev_action, prev_state, gru_Wih, gru_Whh, gru_bih, gru_bhh):
    hp = f64(prev_state)
    xg = np.concatenate([f64(sample), f64(prev_action)], axis=-1)
    gi = xg @ f64(gru_Wih).T + f64(gru_bih)
    gh = hp @ f64(gru_Whh).T + f64(gru_bhh)
    r = sigmoid(gi[:, :H] + gh[:, :H])
    z = sigmoid(gi[:, H:2 * H] + gh[:, H:2 * H])
    ghn = gh[:, 2 * H:]
    n = np.tanh(gi[:, 2 * H:] + r * ghn)
    belief = (1.0 - z) * n + z * hp
    return r, z, n, ghn, belief


def setup_inputs():
    s = mx_kscale(B)[:, None]
    sample = bf(np.random.standard_normal((B, L)) * 1.1)
    prev_action = bf(np.random.standard_normal((B, A)))
    hp0 = bf(np.random.standard_normal((B, S)))
    gru_Wih = bf(np.random.standard_normal((3 * H, G)) / np.sqrt(G))
    gru_Whh = bf(np.random.standard_normal((3 * H, H)) / np.sqrt(H))
    gru_bih = bf(np.random.standard_normal(3 * H) * 0.1)
    gru_bhh = bf(np.random.standard_normal(3 * H) * 0.1)
    g = bf(np.random.standard_normal((B, H)) * np.exp2(np.random.randint(-12, 1, (B, 1))) * 4.0 / s)
    r, z, n, ghn, belief = cell(sample, prev_action, hp0, gru_Wih, gru_Whh, gru_bih, gru_bhh)
    gates = np.concatenate([r, z, n], axis=1)
    return {"sample": sample,
            "prev_action": prev_action,
            "prev_state": bf(f64(hp0) * s),
            "gru_Wih": gru_Wih,
            "gru_Whh": gru_Whh,
            "gru_bih": gru_bih,
            "gru_bhh": gru_bhh,
            "gates": np.asarray(gates, np.float32),
            "gh_n": np.asarray(ghn, np.float32),
            "belief": np.asarray(belief, np.float32),
            "grad_out": g}


def reference(sample, prev_action, prev_state, gru_Wih, gru_Whh, gru_bih, gru_bhh, gates, gh_n, belief, grad_out):
    g = f64(grad_out)
    gt = f64(gates)
    r, z, n = gt[:, :H], gt[:, H:2 * H], gt[:, 2 * H:]
    da = g * (1.0 - z) * (1.0 - n * n)
    d_r = da * f64(gh_n) * r * (1.0 - r)
    d_z = g * (f64(belief) - n) * (1.0 - z)
    d_n = da * r
    dgh = np.concatenate([d_r, d_z, d_n], axis=1)
    return mxq(dgh, 0, "e5m2").T @ mxq(f64(prev_state), 0, "e4m3")

@@ -1,0 +1,219 @@
+import concourse.mybir as mybir
+
+F32 = mybir.dt.float32
+BF16 = mybir.dt.bfloat16
+U32 = mybir.dt.uint32
+U8 = mybir.dt.uint8
+E4M3_X4 = mybir.dt.float8_e4m3fn_x4
+E5M2_X4 = mybir.dt.float8_e5m2_x4
+ALU = mybir.AluOpType
+ACT = mybir.ActivationFunctionType
+
+P = 128
+PACK = 4
+TOKENS = P * PACK
+H = 1024
+M_TILE = 128
+N_TILE = 512
+HALF = H // 2
+CHUNK = 256
+VECTOR_SHARE = 3
+RUN = 4
+
+R_COL, Z_COL, N_COL = 0, H, 2 * H
+
+FLOPS = 2 * TOKENS * 3 * H * H
+BYTES = TOKENS * H * (3 * 4 + 4 + 4 + 2 + 2) + 3 * H * H * 4
+
+
+def by_partition(dram):
+    return dram.rearrange("(p t) w -> p t w", t=PACK)
+
+
+def token_major(ap):
+    return ap.rearrange("p t (c i) -> p c t i", i=RUN)
+
+
+def column_major(ap):
+    return ap.rearrange("p (c i) t -> p c t i", i=RUN)
+
+
+def tile_rssm_pb_v_kernel(
+    tc,
+    sample,
+    prev_action,
+    prev_state,
+    gru_Wih,
+    gru_Whh,
+    gru_bih,
+    gru_bhh,
+    gates,
+    gh_n,
+    belief,
+    grad_out,
+    out,
+):
+    nc = tc.nc
+    with (
+        tc.tile_pool(name="resident", bufs=1) as resident,
+        tc.tile_pool(name="slices", bufs=2) as slices,
+        tc.tile_pool(name="chunks", bufs=4) as chunks,
+        tc.tile_pool(name="rows", bufs=8) as rows,
+        tc.psum_pool(name="banks", bufs=8) as banks,
+    ):
+        state_raw = resident.tile([P, PACK, H], BF16)
+        nc.sync.dma_start(out=state_raw[:], in_=by_partition(prev_state))
+        grad = resident.tile([P, PACK, H], BF16)
+        nc.sync.dma_start(out=grad[:], in_=by_partition(grad_out))
+        gate_rows = resident.tile([P, PACK, 3 * H], F32)
+        for t in range(PACK):
+            nc.sync.dma_start(out=gate_rows[:, t, :], in_=by_partition(gates)[:, t, :])
+        cand = resident.tile([P, PACK, H], F32)
+        nc.sync.dma_start(out=cand[:], in_=by_partition(gh_n))
+        new_state = resident.tile([P, PACK, H], F32)
+        nc.sync.dma_start(out=new_state[:], in_=by_partition(belief))
+
+        state_grouped = resident.tile([P, H, PACK], BF16, align_bytes=64)
+        for first in range(0, H, HALF):
+            cols = slice(first, first + HALF)
+            nc.vector.tensor_copy(
+                out=column_major(state_grouped[:, cols, :]),
+                in_=token_major(state_raw[:, :, cols]),
+            )
+        state_codes = resident.tile([P, H], U32, align_bytes=64)
+        state_scales = resident.tile([P, H], U8, align_bytes=64)
+        nc.vector.quantize_mx(
+            out=state_codes[:].bitcast(E4M3_X4),
+            scales=state_scales[:],
+            in_=state_grouped[:].rearrange("p w t -> p (w t)"),
+        )
+
+        minus_gz = resident.tile([P, PACK, H], F32)
+        minus_dn = resident.tile([P, PACK, H], F32)
+        halves = [0, HALF]
+        for t in range(PACK):
+            n_squared = slices.tile([P, H], F32)
+            da = slices.tile([P, H], F32)
+            nc.scalar.activation(
+                out=n_squared[:], in_=gate_rows[:, t, N_COL : N_COL + H], func=ACT.Square
+            )
+            for a in halves:
+                nc.vector.scalar_tensor_tensor(
+                    out=minus_gz[:, t, a : a + HALF],
+                    in0=gate_rows[:, t, Z_COL + a : Z_COL + a + HALF],
+                    scalar=1.0,
+                    in1=grad[:, t, a : a + HALF],
+                    op0=ALU.subtract,
+                    op1=ALU.mult,
+                )
+            for a in halves:
+                nc.vector.scalar_tensor_tensor(
+                    out=da[:, a : a + HALF],
+                    in0=n_squared[:, a : a + HALF],
+                    scalar=1.0,
+                    in1=minus_gz[:, t, a : a + HALF],
+                    op0=ALU.subtract,
+                    op1=ALU.mult,
+                )
+            for a in halves:
+                nc.vector.scalar_tensor_tensor(
+                    out=minus_dn[:, t, a : a + HALF],
+                    in0=da[:, a : a + HALF],
+                    scalar=-1.0,
+                    in1=gate_rows[:, t, R_COL + a : R_COL + a + HALF],
+                    op0=ALU.mult,
+                    op1=ALU.mult,
+                )
+
+        def multiply_and_store(grouped, first_row):
+            codes = chunks.tile([P, CHUNK], U32, align_bytes=64)
+            scales = chunks.tile([P, CHUNK], U8, align_bytes=64)
+            nc.vector.quantize_mx(
+                out=codes[:].bitcast(E5M2_X4),
+                scales=scales[:],
+                in_=grouped[:].rearrange("p w t -> p (w t)"),
+            )
+            for m in range(0, CHUNK, M_TILE):
+                m_cols = slice(m, m + M_TILE)
+                result = rows.tile([M_TILE, H], F32)
+                for n in range(0, H, N_TILE):
+                    n_cols = slice(n, n + N_TILE)
+                    acc = banks.tile([M_TILE, N_TILE], F32)
+                    nc.tensor.matmul_mx(
+                        out=acc[:],
+                        lhsT=codes[:, m_cols].bitcast(E5M2_X4),
+                        lhsT_scale=scales[:, m_cols],
+                        rhs=state_codes[:, n_cols].bitcast(E4M3_X4),
+                        rhs_scale=state_scales[:, n_cols],
+                        start=True,
+                        stop=True,
+                    )
+                    if n + N_TILE == H and ((first_row + m) // M_TILE) % VECTOR_SHARE == VECTOR_SHARE - 1:
+                        nc.vector.tensor_copy(out=result[:, n_cols], in_=acc[:])
+                    else:
+                        nc.scalar.copy(out=result[:, n_cols], in_=acc[:])
+                nc.sync.dma_start(
+                    out=out[first_row + m : first_row + m + M_TILE, :], in_=result[:]
+                )
+
+        chunk_pairs = [[a, a + CHUNK] for a in range(0, H, 2 * CHUNK)]
+
+        for pair in chunk_pairs:
+            for a in pair:
+                dn_grouped = chunks.tile([P, CHUNK, PACK], BF16, tag="grouped", align_bytes=64)
+                nc.scalar.mul(
+                    out=column_major(dn_grouped[:]),
+                    in_=token_major(minus_dn[:, :, a : a + CHUNK]),
+                    mul=-1.0,
+                )
+                multiply_and_store(dn_grouped, N_COL + a)
+
+        for pair in chunk_pairs:
+            factors = []
+            for a in pair:
+                reset_factor = chunks.tile([P, PACK, CHUNK], F32, tag="factor")
+                nc.vector.scalar_tensor_tensor(
+                    out=reset_factor[:],
+                    in0=gate_rows[:, :, R_COL + a : R_COL + a + CHUNK],
+                    scalar=1.0,
+                    in1=cand[:, :, a : a + CHUNK],
+                    op0=ALU.subtract,
+                    op1=ALU.mult,
+                )
+                factors.append(reset_factor)
+            products = []
+            for a, reset_factor in zip(pair, factors):
+                dr_grouped = chunks.tile([P, CHUNK, PACK], BF16, tag="grouped", align_bytes=64)
+                nc.vector.tensor_tensor(
+                    out=column_major(dr_grouped[:]),
+                    in0=token_major(minus_dn[:, :, a : a + CHUNK]),
+                    in1=token_major(reset_factor[:]),
+                    op=ALU.mult,
+                )
+                products.append(dr_grouped)
+            for a, dr_grouped in zip(pair, products):
+                multiply_and_store(dr_grouped, R_COL + a)
+
+        for pair in chunk_pairs:
+            factors = []
+            for a in pair:
+                update_factor = chunks.tile([P, PACK, CHUNK], F32, tag="factor")
+                nc.vector.tensor_tensor(
+                    out=update_factor[:],
+                    in0=gate_rows[:, :, N_COL + a : N_COL + a + CHUNK],
+                    in1=new_state[:, :, a : a + CHUNK],
+                    op=ALU.subtract,
+                )
+                factors.append(update_factor)
+            products = []
+            for a, update_factor in zip(pair, factors):
+                dz_grouped = chunks.tile([P, CHUNK, PACK], BF16, tag="grouped", align_bytes=64)
+                nc.vector.tensor_tensor(
+                    out=column_major(dz_grouped[:]),
+                    in0=token_major(minus_gz[:, :, a : a + CHUNK]),
+                    in1=token_major(update_factor[:]),
+                    op=ALU.mult,
+                )
+                products.append(dz_grouped)
+            for a, dz_grouped in zip(pair, products):
+                multiply_and_store(dz_grouped, Z_COL + a)

@@ -17,7 +17,6 @@ M_TILE = 128
 N_TILE = 512
 HALF = H // 2
 CHUNK = 256
-VECTOR_SHARE = 3
 RUN = 4
 
 R_COL, Z_COL, N_COL = 0, H, 2 * H
@@ -148,10 +147,7 @@ def tile_rssm_pb_v_kernel(
                         start=True,
                         stop=True,
                     )
-                    if n + N_TILE == H and ((first_row + m) // M_TILE) % VECTOR_SHARE == VECTOR_SHARE - 1:
-                        nc.vector.tensor_copy(out=result[:, n_cols], in_=acc[:])
-                    else:
-                        nc.scalar.copy(out=result[:, n_cols], in_=acc[:])
+                    nc.scalar.copy(out=result[:, n_cols], in_=acc[:])
                 nc.sync.dma_start(
                     out=out[first_row + m : first_row + m + M_TILE, :], in_=result[:]
                 )
@@ -159,13 +155,18 @@ def tile_rssm_pb_v_kernel(
         chunk_pairs = [[a, a + CHUNK] for a in range(0, H, 2 * CHUNK)]
 
         for pair in chunk_pairs:
+            products = []
             for a in pair:
                 dn_grouped = chunks.tile([P, CHUNK, PACK], BF16, tag="grouped", align_bytes=64)
-                nc.scalar.mul(
+                nc.vector.tensor_scalar(
                     out=column_major(dn_grouped[:]),
-                    in_=token_major(minus_dn[:, :, a : a + CHUNK]),
-                    mul=-1.0,
+                    in0=token_major(minus_dn[:, :, a : a + CHUNK]),
+                    scalar1=-1.0,
+                    scalar2=None,
+                    op0=ALU.mult,
                 )
+                products.append(dn_grouped)
+            for a, dn_grouped in zip(pair, products):
                 multiply_and_store(dn_grouped, N_COL + a)
 
         for pair in chunk_pairs:

@@ -18,6 +18,7 @@ N_TILE = 512
 HALF = H // 2
 CHUNK = 256
 RUN = 4
+TILES = CHUNK // M_TILE
 
 R_COL, Z_COL, N_COL = 0, H, 2 * H
 
@@ -35,6 +36,14 @@ def token_major(ap):
 
 def column_major(ap):
     return ap.rearrange("p (c i) t -> p c t i", i=RUN)
+
+
+def token_major_dealt(ap):
+    return ap.rearrange("p t (c j) -> p c t j", j=TILES)
+
+
+def column_major_dealt(ap):
+    return ap.rearrange("p (j c) t -> p c t j", j=TILES)
 
 
 def tile_rssm_pb_v_kernel(
@@ -57,7 +66,7 @@ def tile_rssm_pb_v_kernel(
         tc.tile_pool(name="resident", bufs=1) as resident,
         tc.tile_pool(name="slices", bufs=2) as slices,
         tc.tile_pool(name="chunks", bufs=4) as chunks,
-        tc.tile_pool(name="rows", bufs=8) as rows,
+        tc.tile_pool(name="rows", bufs=4) as rows,
         tc.psum_pool(name="banks", bufs=8) as banks,
     ):
         state_raw = resident.tile([P, PACK, H], BF16)
@@ -124,7 +133,10 @@ def tile_rssm_pb_v_kernel(
                     op1=ALU.mult,
                 )
 
-        def multiply_and_store(grouped, first_row):
+        def multiply_and_store(grouped, first_row, tile_by_tile=False):
+            rows_of_chunk = out[first_row : first_row + CHUNK, :].rearrange(
+                "(p j) n -> p j n", j=TILES
+            )
             codes = chunks.tile([P, CHUNK], U32, align_bytes=64)
             scales = chunks.tile([P, CHUNK], U8, align_bytes=64)
             nc.vector.quantize_mx(
@@ -132,9 +144,9 @@ def tile_rssm_pb_v_kernel(
                 scales=scales[:],
                 in_=grouped[:].rearrange("p w t -> p (w t)"),
             )
-            for m in range(0, CHUNK, M_TILE):
-                m_cols = slice(m, m + M_TILE)
-                result = rows.tile([M_TILE, H], F32)
+            result = rows.tile([M_TILE, TILES, H], F32)
+            for j in range(TILES):
+                m_cols = slice(j * M_TILE, (j + 1) * M_TILE)
                 for n in range(0, H, N_TILE):
                     n_cols = slice(n, n + N_TILE)
                     acc = banks.tile([M_TILE, N_TILE], F32)
@@ -147,10 +159,11 @@ def tile_rssm_pb_v_kernel(
                         start=True,
                         stop=True,
                     )
-                    nc.scalar.copy(out=result[:, n_cols], in_=acc[:])
-                nc.sync.dma_start(
-                    out=out[first_row + m : first_row + m + M_TILE, :], in_=result[:]
-                )
+                    nc.scalar.copy(out=result[:, j, n_cols], in_=acc[:])
+                if tile_by_tile:
+                    nc.sync.dma_start(out=rows_of_chunk[:, j, :], in_=result[:, j, :])
+            if not tile_by_tile:
+                nc.sync.dma_start(out=rows_of_chunk, in_=result[:])
 
         chunk_pairs = [[a, a + CHUNK] for a in range(0, H, 2 * CHUNK)]
 
@@ -159,15 +172,15 @@ def tile_rssm_pb_v_kernel(
             for a in pair:
                 dn_grouped = chunks.tile([P, CHUNK, PACK], BF16, tag="grouped", align_bytes=64)
                 nc.vector.tensor_scalar(
-                    out=column_major(dn_grouped[:]),
-                    in0=token_major(minus_dn[:, :, a : a + CHUNK]),
+                    out=column_major_dealt(dn_grouped[:]),
+                    in0=token_major_dealt(minus_dn[:, :, a : a + CHUNK]),
                     scalar1=-1.0,
                     scalar2=None,
                     op0=ALU.mult,
                 )
                 products.append(dn_grouped)
             for a, dn_grouped in zip(pair, products):
-                multiply_and_store(dn_grouped, N_COL + a)
+                multiply_and_store(dn_grouped, N_COL + a, tile_by_tile=(a == 0))
 
         for pair in chunk_pairs:
             factors = []
@@ -186,9 +199,9 @@ def tile_rssm_pb_v_kernel(
             for a, reset_factor in zip(pair, factors):
                 dr_grouped = chunks.tile([P, CHUNK, PACK], BF16, tag="grouped", align_bytes=64)
                 nc.vector.tensor_tensor(
-                    out=column_major(dr_grouped[:]),
-                    in0=token_major(minus_dn[:, :, a : a + CHUNK]),
-                    in1=token_major(reset_factor[:]),
+                    out=column_major_dealt(dr_grouped[:]),
+                    in0=token_major_dealt(minus_dn[:, :, a : a + CHUNK]),
+                    in1=token_major_dealt(reset_factor[:]),
                     op=ALU.mult,
                 )
                 products.append(dr_grouped)
@@ -210,11 +223,11 @@ def tile_rssm_pb_v_kernel(
             for a, update_factor in zip(pair, factors):
                 dz_grouped = chunks.tile([P, CHUNK, PACK], BF16, tag="grouped", align_bytes=64)
                 nc.vector.tensor_tensor(
-                    out=column_major(dz_grouped[:]),
-                    in0=token_major(minus_gz[:, :, a : a + CHUNK]),
-                    in1=token_major(update_factor[:]),
+                    out=column_major_dealt(dz_grouped[:]),
+                    in0=token_major_dealt(minus_gz[:, :, a : a + CHUNK]),
+                    in1=token_major_dealt(update_factor[:]),
                     op=ALU.mult,
                 )
                 products.append(dz_grouped)
             for a, dz_grouped in zip(pair, products):
-                multiply_and_store(dz_grouped, Z_COL + a)
+                multiply_and_store(dz_grouped, Z_COL + a, tile_by_tile=(a == H - CHUNK))

@@ -64,9 +64,8 @@ def tile_rssm_pb_v_kernel(
     nc = tc.nc
     with (
         tc.tile_pool(name="resident", bufs=1) as resident,
-        tc.tile_pool(name="slices", bufs=2) as slices,
         tc.tile_pool(name="chunks", bufs=4) as chunks,
-        tc.tile_pool(name="rows", bufs=4) as rows,
+        tc.tile_pool(name="rows", bufs=5) as rows,
         tc.psum_pool(name="banks", bufs=8) as banks,
     ):
         state_raw = resident.tile([P, PACK, H], BF16)
@@ -75,7 +74,14 @@ def tile_rssm_pb_v_kernel(
         nc.sync.dma_start(out=grad[:], in_=by_partition(grad_out))
         gate_rows = resident.tile([P, PACK, 3 * H], F32)
         for t in range(PACK):
-            nc.sync.dma_start(out=gate_rows[:, t, :], in_=by_partition(gates)[:, t, :])
+            nc.sync.dma_start(
+                out=gate_rows[:, t, Z_COL : 3 * H], in_=by_partition(gates)[:, t, Z_COL : 3 * H]
+            )
+        for t in range(PACK):
+            nc.sync.dma_start(
+                out=gate_rows[:, t, R_COL : R_COL + H],
+                in_=by_partition(gates)[:, t, R_COL : R_COL + H],
+            )
         cand = resident.tile([P, PACK, H], F32)
         nc.sync.dma_start(out=cand[:], in_=by_partition(gh_n))
         new_state = resident.tile([P, PACK, H], F32)
@@ -96,18 +102,15 @@ def tile_rssm_pb_v_kernel(
             in_=state_grouped[:].rearrange("p w t -> p (w t)"),
         )
 
-        minus_gz = resident.tile([P, PACK, H], F32)
-        minus_dn = resident.tile([P, PACK, H], F32)
+        da = resident.tile([P, PACK, H], F32)
         halves = [0, HALF]
         for t in range(PACK):
-            n_squared = slices.tile([P, H], F32)
-            da = slices.tile([P, H], F32)
             nc.scalar.activation(
-                out=n_squared[:], in_=gate_rows[:, t, N_COL : N_COL + H], func=ACT.Square
+                out=da[:, t, :], in_=gate_rows[:, t, N_COL : N_COL + H], func=ACT.Square
             )
             for a in halves:
                 nc.vector.scalar_tensor_tensor(
-                    out=minus_gz[:, t, a : a + HALF],
+                    out=gate_rows[:, t, Z_COL + a : Z_COL + a + HALF],
                     in0=gate_rows[:, t, Z_COL + a : Z_COL + a + HALF],
                     scalar=1.0,
                     in1=grad[:, t, a : a + HALF],
@@ -116,27 +119,81 @@ def tile_rssm_pb_v_kernel(
                 )
             for a in halves:
                 nc.vector.scalar_tensor_tensor(
-                    out=da[:, a : a + HALF],
-                    in0=n_squared[:, a : a + HALF],
+                    out=da[:, t, a : a + HALF],
+                    in0=da[:, t, a : a + HALF],
                     scalar=1.0,
-                    in1=minus_gz[:, t, a : a + HALF],
+                    in1=gate_rows[:, t, Z_COL + a : Z_COL + a + HALF],
                     op0=ALU.subtract,
                     op1=ALU.mult,
                 )
-            for a in halves:
-                nc.vector.scalar_tensor_tensor(
-                    out=minus_dn[:, t, a : a + HALF],
-                    in0=da[:, a : a + HALF],
-                    scalar=-1.0,
-                    in1=gate_rows[:, t, R_COL + a : R_COL + a + HALF],
-                    op0=ALU.mult,
-                    op1=ALU.mult,
-                )
 
-        def multiply_and_store(grouped, first_row, tile_by_tile=False):
-            rows_of_chunk = out[first_row : first_row + CHUNK, :].rearrange(
-                "(p j) n -> p j n", j=TILES
+        starts = list(range(0, H, CHUNK))
+        minus_dn = {}
+        for a in starts:
+            minus_dn[a] = resident.tile([P, PACK, CHUNK], F32, name="minus_dn_%d" % a)
+
+        def make_minus_dn(tokens, a):
+            nc.vector.scalar_tensor_tensor(
+                out=minus_dn[a][:, tokens, :],
+                in0=da[:, tokens, a : a + CHUNK],
+                scalar=-1.0,
+                in1=gate_rows[:, tokens, R_COL + a : R_COL + a + CHUNK],
+                op0=ALU.mult,
+                op1=ALU.mult,
             )
+
+        early = slice(0, PACK // 2)
+        late = slice(PACK // 2, PACK)
+        for a in starts:
+            make_minus_dn(early, a)
+
+        def chunk_of(tile_, first):
+            return tile_[:, :, first : first + CHUNK]
+
+        factors = {}
+
+        def make_reset(a):
+            factor = chunks.tile([P, PACK, CHUNK], F32)
+            nc.vector.scalar_tensor_tensor(
+                out=factor[:],
+                in0=chunk_of(gate_rows, R_COL + a),
+                scalar=1.0,
+                in1=chunk_of(cand, a),
+                op0=ALU.subtract,
+                op1=ALU.mult,
+            )
+            factors[R_COL + a] = factor
+
+        def make_update(a):
+            factor = chunks.tile([P, PACK, CHUNK], F32)
+            nc.vector.tensor_tensor(
+                out=factor[:],
+                in0=chunk_of(gate_rows, N_COL + a),
+                in1=chunk_of(new_state, a),
+                op=ALU.subtract,
+            )
+            factors[Z_COL + a] = factor
+
+        def product(in0, in1):
+            grouped = chunks.tile([P, CHUNK, PACK], BF16, align_bytes=64)
+            if in1 is None:
+                nc.vector.tensor_scalar(
+                    out=column_major_dealt(grouped[:]),
+                    in0=token_major_dealt(in0),
+                    scalar1=-1.0,
+                    scalar2=None,
+                    op0=ALU.mult,
+                )
+            else:
+                nc.vector.tensor_tensor(
+                    out=column_major_dealt(grouped[:]),
+                    in0=token_major_dealt(in0),
+                    in1=token_major_dealt(in1),
+                    op=ALU.mult,
+                )
+            return grouped
+
+        def quantise(grouped):
             codes = chunks.tile([P, CHUNK], U32, align_bytes=64)
             scales = chunks.tile([P, CHUNK], U8, align_bytes=64)
             nc.vector.quantize_mx(
@@ -144,11 +201,14 @@ def tile_rssm_pb_v_kernel(
                 scales=scales[:],
                 in_=grouped[:].rearrange("p w t -> p (w t)"),
             )
-            result = rows.tile([M_TILE, TILES, H], F32)
+            return codes, scales
+
+        def multiply(codes, scales):
+            filled = []
             for j in range(TILES):
                 m_cols = slice(j * M_TILE, (j + 1) * M_TILE)
-                for n in range(0, H, N_TILE):
-                    n_cols = slice(n, n + N_TILE)
+                for first in range(0, H, N_TILE):
+                    n_cols = slice(first, first + N_TILE)
                     acc = banks.tile([M_TILE, N_TILE], F32)
                     nc.tensor.matmul_mx(
                         out=acc[:],
@@ -159,75 +219,46 @@ def tile_rssm_pb_v_kernel(
                         start=True,
                         stop=True,
                     )
+                    filled.append((acc, j, n_cols))
+            return filled
+
+        def rows_of_chunk(first_row):
+            return out[first_row : first_row + CHUNK, :].rearrange("(p j) n -> p j n", j=TILES)
+
+        products = (
+            [(minus_dn[a][:], False, N_COL + a) for a in starts]
+            + [(minus_dn[a][:], True, R_COL + a) for a in starts]
+            + [(chunk_of(gate_rows, Z_COL + a), True, Z_COL + a) for a in starts]
+        )
+        preparations = (
+            [lambda a=a: make_minus_dn(late, a) for a in starts]
+            + [lambda a=a: make_reset(a) for a in starts]
+            + [lambda a=a: make_update(a) for a in starts]
+        )
+        preparations[0]()
+        preparations[1]()
+        count = len(products)
+        SHARED = 2
+        per_tile = len(halves)
+        waiting = []
+        for k in range(count):
+            in0, with_factor, first_row = products[k]
+            grouped = product(in0, factors[first_row][:] if with_factor else None)
+            if k + 2 < len(preparations):
+                preparations[k + 2]()
+            codes, scales = quantise(grouped)
+            filled = multiply(codes, scales)
+            result = rows.tile([M_TILE, TILES, H], F32)
+            if k < count - SHARED:
+                for acc, j, n_cols in filled:
                     nc.scalar.copy(out=result[:, j, n_cols], in_=acc[:])
-                if tile_by_tile:
-                    nc.sync.dma_start(out=rows_of_chunk[:, j, :], in_=result[:, j, :])
-            if not tile_by_tile:
-                nc.sync.dma_start(out=rows_of_chunk, in_=result[:])
-
-        chunk_pairs = [[a, a + CHUNK] for a in range(0, H, 2 * CHUNK)]
-
-        for pair in chunk_pairs:
-            products = []
-            for a in pair:
-                dn_grouped = chunks.tile([P, CHUNK, PACK], BF16, tag="grouped", align_bytes=64)
-                nc.vector.tensor_scalar(
-                    out=column_major_dealt(dn_grouped[:]),
-                    in0=token_major_dealt(minus_dn[:, :, a : a + CHUNK]),
-                    scalar1=-1.0,
-                    scalar2=None,
-                    op0=ALU.mult,
-                )
-                products.append(dn_grouped)
-            for a, dn_grouped in zip(pair, products):
-                multiply_and_store(dn_grouped, N_COL + a, tile_by_tile=(a == 0))
-
-        for pair in chunk_pairs:
-            factors = []
-            for a in pair:
-                reset_factor = chunks.tile([P, PACK, CHUNK], F32, tag="factor")
-                nc.vector.scalar_tensor_tensor(
-                    out=reset_factor[:],
-                    in0=gate_rows[:, :, R_COL + a : R_COL + a + CHUNK],
-                    scalar=1.0,
-                    in1=cand[:, :, a : a + CHUNK],
-                    op0=ALU.subtract,
-                    op1=ALU.mult,
-                )
-                factors.append(reset_factor)
-            products = []
-            for a, reset_factor in zip(pair, factors):
-                dr_grouped = chunks.tile([P, CHUNK, PACK], BF16, tag="grouped", align_bytes=64)
-                nc.vector.tensor_tensor(
-                    out=column_major_dealt(dr_grouped[:]),
-                    in0=token_major_dealt(minus_dn[:, :, a : a + CHUNK]),
-                    in1=token_major_dealt(reset_factor[:]),
-                    op=ALU.mult,
-                )
-                products.append(dr_grouped)
-            for a, dr_grouped in zip(pair, products):
-                multiply_and_store(dr_grouped, R_COL + a)
-
-        for pair in chunk_pairs:
-            factors = []
-            for a in pair:
-                update_factor = chunks.tile([P, PACK, CHUNK], F32, tag="factor")
-                nc.vector.tensor_tensor(
-                    out=update_factor[:],
-                    in0=gate_rows[:, :, N_COL + a : N_COL + a + CHUNK],
-                    in1=new_state[:, :, a : a + CHUNK],
-                    op=ALU.subtract,
-                )
-                factors.append(update_factor)
-            products = []
-            for a, update_factor in zip(pair, factors):
-                dz_grouped = chunks.tile([P, CHUNK, PACK], BF16, tag="grouped", align_bytes=64)
-                nc.vector.tensor_tensor(
-                    out=column_major_dealt(dz_grouped[:]),
-                    in0=token_major_dealt(minus_gz[:, :, a : a + CHUNK]),
-                    in1=token_major_dealt(update_factor[:]),
-                    op=ALU.mult,
-                )
-                products.append(dz_grouped)
-            for a, dz_grouped in zip(pair, products):
-                multiply_and_store(dz_grouped, Z_COL + a, tile_by_tile=(a == H - CHUNK))
+                nc.sync.dma_start(out=rows_of_chunk(first_row), in_=result[:])
+            else:
+                for acc, j, n_cols in filled[:per_tile]:
+                    nc.scalar.copy(out=result[:, j, n_cols], in_=acc[:])
+                nc.sync.dma_start(out=rows_of_chunk(first_row)[:, 0, :], in_=result[:, 0, :])
+                waiting.append((filled[per_tile:], result, first_row))
+        for filled, result, first_row in waiting:
+            for acc, j, n_cols in filled:
+                nc.vector.tensor_copy(out=result[:, j, n_cols], in_=acc[:])
+            nc.sync.dma_start(out=rows_of_chunk(first_row)[:, 1, :], in_=result[:, 1, :])

@@ -68,11 +68,11 @@ def tile_rssm_pb_v_kernel(
         tc.tile_pool(name="rows", bufs=5) as rows,
         tc.psum_pool(name="banks", bufs=8) as banks,
     ):
-        state_raw = resident.tile([P, PACK, H], BF16)
+        state_raw = resident.tile([P, PACK, H], BF16, align_bytes=256)
         nc.sync.dma_start(out=state_raw[:], in_=by_partition(prev_state))
-        grad = resident.tile([P, PACK, H], BF16)
+        grad = resident.tile([P, PACK, H], BF16, align_bytes=256)
         nc.sync.dma_start(out=grad[:], in_=by_partition(grad_out))
-        gate_rows = resident.tile([P, PACK, 3 * H], F32)
+        gate_rows = resident.tile([P, PACK, 3 * H], F32, align_bytes=256)
         for t in range(PACK):
             nc.sync.dma_start(
                 out=gate_rows[:, t, Z_COL : 3 * H], in_=by_partition(gates)[:, t, Z_COL : 3 * H]
@@ -82,9 +82,9 @@ def tile_rssm_pb_v_kernel(
                 out=gate_rows[:, t, R_COL : R_COL + H],
                 in_=by_partition(gates)[:, t, R_COL : R_COL + H],
             )
-        cand = resident.tile([P, PACK, H], F32)
+        cand = resident.tile([P, PACK, H], F32, align_bytes=256)
         nc.sync.dma_start(out=cand[:], in_=by_partition(gh_n))
-        new_state = resident.tile([P, PACK, H], F32)
+        new_state = resident.tile([P, PACK, H], F32, align_bytes=256)
         nc.sync.dma_start(out=new_state[:], in_=by_partition(belief))
 
         state_grouped = resident.tile([P, H, PACK], BF16, align_bytes=64)
@@ -248,7 +248,7 @@ def tile_rssm_pb_v_kernel(
                 preparations[k + 2]()
             codes, scales = quantise(grouped)
             filled = multiply(codes, scales)
-            result = rows.tile([M_TILE, TILES, H], F32)
+            result = rows.tile([M_TILE, TILES, H], F32, align_bytes=256)
             if k < count - SHARED:
                 for acc, j, n_cols in filled:
                     nc.scalar.copy(out=result[:, j, n_cols], in_=acc[:])

@@ -67,6 +67,7 @@ def tile_rssm_pb_v_kernel(
         tc.tile_pool(name="chunks", bufs=4) as chunks,
         tc.tile_pool(name="rows", bufs=5) as rows,
         tc.psum_pool(name="banks", bufs=8) as banks,
+        tc.manual_schedule(engines={mybir.EngineType.DVE}),
     ):
         state_raw = resident.tile([P, PACK, H], BF16, align_bytes=256)
         nc.sync.dma_start(out=state_raw[:], in_=by_partition(prev_state))
@@ -77,10 +78,10 @@ def tile_rssm_pb_v_kernel(
             nc.sync.dma_start(
                 out=gate_rows[:, t, Z_COL : 3 * H], in_=by_partition(gates)[:, t, Z_COL : 3 * H]
             )
-        for t in range(PACK):
+        for t in range(0, PACK, 2):
             nc.sync.dma_start(
-                out=gate_rows[:, t, R_COL : R_COL + H],
-                in_=by_partition(gates)[:, t, R_COL : R_COL + H],
+                out=gate_rows[:, t : t + 2, R_COL : R_COL + H],
+                in_=by_partition(gates)[:, t : t + 2, R_COL : R_COL + H],
             )
         cand = resident.tile([P, PACK, H], F32, align_bytes=256)
         nc.sync.dma_start(out=cand[:], in_=by_partition(gh_n))
@@ -144,8 +145,6 @@ def tile_rssm_pb_v_kernel(
 
         early = slice(0, PACK // 2)
         late = slice(PACK // 2, PACK)
-        for a in starts:
-            make_minus_dn(early, a)
 
         def chunk_of(tile_, first):
             return tile_[:, :, first : first + CHUNK]
@@ -230,13 +229,18 @@ def tile_rssm_pb_v_kernel(
             + [(minus_dn[a][:], True, R_COL + a) for a in starts]
             + [(chunk_of(gate_rows, Z_COL + a), True, Z_COL + a) for a in starts]
         )
+        for a in starts[:3]:
+            make_minus_dn(early, a)
+        for a in starts[:2]:
+            make_minus_dn(late, a)
         preparations = (
-            [lambda a=a: make_minus_dn(late, a) for a in starts]
-            + [lambda a=a: make_reset(a) for a in starts]
-            + [lambda a=a: make_update(a) for a in starts]
+            [
+                [lambda: make_minus_dn(early, starts[3])],
+                [lambda: make_minus_dn(late, starts[2]), lambda: make_minus_dn(late, starts[3])],
+            ]
+            + [[lambda a=a: make_reset(a)] for a in starts]
+            + [[lambda a=a: make_update(a)] for a in starts]
         )
-        preparations[0]()
-        preparations[1]()
         count = len(products)
         SHARED = 2
         per_tile = len(halves)
@@ -244,8 +248,9 @@ def tile_rssm_pb_v_kernel(
         for k in range(count):
             in0, with_factor, first_row = products[k]
             grouped = product(in0, factors[first_row][:] if with_factor else None)
-            if k + 2 < len(preparations):
-                preparations[k + 2]()
+            if k < len(preparations):
+                for prepare in preparations[k]:
+                    prepare()
             codes, scales = quantise(grouped)
             filled = multiply(codes, scales)
             result = rows.tile([M_TILE, TILES, H], F32, align_bytes=256)
@@ -256,9 +261,8 @@ def tile_rssm_pb_v_kernel(
             else:
                 for acc, j, n_cols in filled[:per_tile]:
                     nc.scalar.copy(out=result[:, j, n_cols], in_=acc[:])
-                nc.sync.dma_start(out=rows_of_chunk(first_row)[:, 0, :], in_=result[:, 0, :])
                 waiting.append((filled[per_tile:], result, first_row))
         for filled, result, first_row in waiting:
             for acc, j, n_cols in filled:
                 nc.vector.tensor_copy(out=result[:, j, n_cols], in_=acc[:])
-            nc.sync.dma_start(out=rows_of_chunk(first_row)[:, 1, :], in_=result[:, 1, :])
+            nc.sync.dma_start(out=rows_of_chunk(first_row), in_=result[:])

@@ -257,7 +257,8 @@ def tile_rssm_pb_v_kernel(
             if k < count - SHARED:
                 for acc, j, n_cols in filled:
                     nc.scalar.copy(out=result[:, j, n_cols], in_=acc[:])
-                nc.sync.dma_start(out=rows_of_chunk(first_row), in_=result[:])
+                queue = nc.scalar if k % 2 == 0 else nc.sync
+                queue.dma_start(out=rows_of_chunk(first_row), in_=result[:])
             else:
                 for acc, j, n_cols in filled[:per_tile]:
                     nc.scalar.copy(out=result[:, j, n_cols], in_=acc[:])

@@ -254,7 +254,14 @@ def tile_rssm_pb_v_kernel(
             codes, scales = quantise(grouped)
             filled = multiply(codes, scales)
             result = rows.tile([M_TILE, TILES, H], F32, align_bytes=256)
-            if k < count - SHARED:
+            if k == 0:
+                for acc, j, n_cols in filled[:per_tile]:
+                    nc.scalar.copy(out=result[:, j, n_cols], in_=acc[:])
+                nc.scalar.dma_start(out=rows_of_chunk(first_row)[:, 0, :], in_=result[:, 0, :])
+                for acc, j, n_cols in filled[per_tile:]:
+                    nc.scalar.copy(out=result[:, j, n_cols], in_=acc[:])
+                nc.sync.dma_start(out=rows_of_chunk(first_row)[:, 1, :], in_=result[:, 1, :])
+            elif k < count - SHARED:
                 for acc, j, n_cols in filled:
                     nc.scalar.copy(out=result[:, j, n_cols], in_=acc[:])
                 queue = nc.scalar if k % 2 == 0 else nc.sync

@@ -260,12 +260,11 @@ def tile_rssm_pb_v_kernel(
                 nc.scalar.dma_start(out=rows_of_chunk(first_row)[:, 0, :], in_=result[:, 0, :])
                 for acc, j, n_cols in filled[per_tile:]:
                     nc.scalar.copy(out=result[:, j, n_cols], in_=acc[:])
-                nc.sync.dma_start(out=rows_of_chunk(first_row)[:, 1, :], in_=result[:, 1, :])
+                nc.scalar.dma_start(out=rows_of_chunk(first_row)[:, 1, :], in_=result[:, 1, :])
             elif k < count - SHARED:
                 for acc, j, n_cols in filled:
                     nc.scalar.copy(out=result[:, j, n_cols], in_=acc[:])
-                queue = nc.scalar if k % 2 == 0 else nc.sync
-                queue.dma_start(out=rows_of_chunk(first_row), in_=result[:])
+                nc.scalar.dma_start(out=rows_of_chunk(first_row), in_=result[:])
             else:
                 for acc, j, n_cols in filled[:per_tile]:
                     nc.scalar.copy(out=result[:, j, n_cols], in_=acc[:])

@@ -272,4 +272,4 @@ def tile_rssm_pb_v_kernel(
         for filled, result, first_row in waiting:
             for acc, j, n_cols in filled:
                 nc.vector.tensor_copy(out=result[:, j, n_cols], in_=acc[:])
-            nc.sync.dma_start(out=rows_of_chunk(first_row), in_=result[:])
+            nc.scalar.dma_start(out=rows_of_chunk(first_row), in_=result[:])

@@ -69,11 +69,11 @@ def tile_rssm_pb_v_kernel(
         tc.psum_pool(name="banks", bufs=8) as banks,
         tc.manual_schedule(engines={mybir.EngineType.DVE}),
     ):
-        state_raw = resident.tile([P, PACK, H], BF16, align_bytes=256)
+        state_raw = resident.tile([P, PACK, H], BF16, align_bytes=4096)
         nc.sync.dma_start(out=state_raw[:], in_=by_partition(prev_state))
-        grad = resident.tile([P, PACK, H], BF16, align_bytes=256)
+        grad = resident.tile([P, PACK, H], BF16, align_bytes=4096)
         nc.sync.dma_start(out=grad[:], in_=by_partition(grad_out))
-        gate_rows = resident.tile([P, PACK, 3 * H], F32, align_bytes=256)
+        gate_rows = resident.tile([P, PACK, 3 * H], F32, align_bytes=4096)
         for t in range(PACK):
             nc.sync.dma_start(
                 out=gate_rows[:, t, Z_COL : 3 * H], in_=by_partition(gates)[:, t, Z_COL : 3 * H]
@@ -83,9 +83,9 @@ def tile_rssm_pb_v_kernel(
                 out=gate_rows[:, t : t + 2, R_COL : R_COL + H],
                 in_=by_partition(gates)[:, t : t + 2, R_COL : R_COL + H],
             )
-        cand = resident.tile([P, PACK, H], F32, align_bytes=256)
+        cand = resident.tile([P, PACK, H], F32, align_bytes=4096)
         nc.sync.dma_start(out=cand[:], in_=by_partition(gh_n))
-        new_state = resident.tile([P, PACK, H], F32, align_bytes=256)
+        new_state = resident.tile([P, PACK, H], F32, align_bytes=4096)
         nc.sync.dma_start(out=new_state[:], in_=by_partition(belief))
 
         state_grouped = resident.tile([P, H, PACK], BF16, align_bytes=64)
@@ -253,7 +253,7 @@ def tile_rssm_pb_v_kernel(
                     prepare()
             codes, scales = quantise(grouped)
             filled = multiply(codes, scales)
-            result = rows.tile([M_TILE, TILES, H], F32, align_bytes=256)
+            result = rows.tile([M_TILE, TILES, H], F32, align_bytes=4096)
             if k == 0:
                 for acc, j, n_cols in filled[:per_tile]:
                     nc.scalar.copy(out=result[:, j, n_cols], in_=acc[:])

import concourse.mybir as mybir

F32 = mybir.dt.float32
BF16 = mybir.dt.bfloat16
U32 = mybir.dt.uint32
U8 = mybir.dt.uint8
E4M3_X4 = mybir.dt.float8_e4m3fn_x4
E5M2_X4 = mybir.dt.float8_e5m2_x4
ALU = mybir.AluOpType
ACT = mybir.ActivationFunctionType

P = 128
PACK = 4
TOKENS = P * PACK
H = 1024
M_TILE = 128
N_TILE = 512
HALF = H // 2
CHUNK = 256
RUN = 4
TILES = CHUNK // M_TILE

R_COL, Z_COL, N_COL = 0, H, 2 * H

FLOPS = 2 * TOKENS * 3 * H * H
BYTES = TOKENS * H * (3 * 4 + 4 + 4 + 2 + 2) + 3 * H * H * 4


def by_partition(dram):
    return dram.rearrange("(p t) w -> p t w", t=PACK)


def token_major(ap):
    return ap.rearrange("p t (c i) -> p c t i", i=RUN)


def column_major(ap):
    return ap.rearrange("p (c i) t -> p c t i", i=RUN)


def token_major_dealt(ap):
    return ap.rearrange("p t (c j) -> p c t j", j=TILES)


def column_major_dealt(ap):
    return ap.rearrange("p (j c) t -> p c t j", j=TILES)


def tile_rssm_pb_v_kernel(
    tc,
    sample,
    prev_action,
    prev_state,
    gru_Wih,
    gru_Whh,
    gru_bih,
    gru_bhh,
    gates,
    gh_n,
    belief,
    grad_out,
    out,
):
    nc = tc.nc
    with (
        tc.tile_pool(name="resident", bufs=1) as resident,
        tc.tile_pool(name="chunks", bufs=4) as chunks,
        tc.tile_pool(name="rows", bufs=5) as rows,
        tc.psum_pool(name="banks", bufs=8) as banks,
        tc.manual_schedule(engines={mybir.EngineType.DVE}),
    ):
        state_raw = resident.tile([P, PACK, H], BF16, align_bytes=4096)
        nc.sync.dma_start(out=state_raw[:], in_=by_partition(prev_state))
        grad = resident.tile([P, PACK, H], BF16, align_bytes=4096)
        nc.sync.dma_start(out=grad[:], in_=by_partition(grad_out))
        gate_rows = resident.tile([P, PACK, 3 * H], F32, align_bytes=4096)
        for t in range(PACK):
            nc.sync.dma_start(
                out=gate_rows[:, t, Z_COL : 3 * H], in_=by_partition(gates)[:, t, Z_COL : 3 * H]
            )
        for t in range(0, PACK, 2):
            nc.sync.dma_start(
                out=gate_rows[:, t : t + 2, R_COL : R_COL + H],
                in_=by_partition(gates)[:, t : t + 2, R_COL : R_COL + H],
            )
        cand = resident.tile([P, PACK, H], F32, align_bytes=4096)
        nc.sync.dma_start(out=cand[:], in_=by_partition(gh_n))
        new_state = resident.tile([P, PACK, H], F32, align_bytes=4096)
        nc.sync.dma_start(out=new_state[:], in_=by_partition(belief))

        state_grouped = resident.tile([P, H, PACK], BF16, align_bytes=64)
        for first in range(0, H, HALF):
            cols = slice(first, first + HALF)
            nc.vector.tensor_copy(
                out=column_major(state_grouped[:, cols, :]),
                in_=token_major(state_raw[:, :, cols]),
            )
        state_codes = resident.tile([P, H], U32, align_bytes=64)
        state_scales = resident.tile([P, H], U8, align_bytes=64)
        nc.vector.quantize_mx(
            out=state_codes[:].bitcast(E4M3_X4),
            scales=state_scales[:],
            in_=state_grouped[:].rearrange("p w t -> p (w t)"),
        )

        da = resident.tile([P, PACK, H], F32)
        halves = [0, HALF]
        for t in range(PACK):
            nc.scalar.activation(
                out=da[:, t, :], in_=gate_rows[:, t, N_COL : N_COL + H], func=ACT.Square
            )
            for a in halves:
                nc.vector.scalar_tensor_tensor(
                    out=gate_rows[:, t, Z_COL + a : Z_COL + a + HALF],
                    in0=gate_rows[:, t, Z_COL + a : Z_COL + a + HALF],
                    scalar=1.0,
                    in1=grad[:, t, a : a + HALF],
                    op0=ALU.subtract,
                    op1=ALU.mult,
                )
            for a in halves:
                nc.vector.scalar_tensor_tensor(
                    out=da[:, t, a : a + HALF],
                    in0=da[:, t, a : a + HALF],
                    scalar=1.0,
                    in1=gate_rows[:, t, Z_COL + a : Z_COL + a + HALF],
                    op0=ALU.subtract,
                    op1=ALU.mult,
                )

        starts = list(range(0, H, CHUNK))
        minus_dn = {}
        for a in starts:
            minus_dn[a] = resident.tile([P, PACK, CHUNK], F32, name="minus_dn_%d" % a)

        def make_minus_dn(tokens, a):
            nc.vector.scalar_tensor_tensor(
                out=minus_dn[a][:, tokens, :],
                in0=da[:, tokens, a : a + CHUNK],
                scalar=-1.0,
                in1=gate_rows[:, tokens, R_COL + a : R_COL + a + CHUNK],
                op0=ALU.mult,
                op1=ALU.mult,
            )

        early = slice(0, PACK // 2)
        late = slice(PACK // 2, PACK)

        def chunk_of(tile_, first):
            return tile_[:, :, first : first + CHUNK]

        factors = {}

        def make_reset(a):
            factor = chunks.tile([P, PACK, CHUNK], F32)
            nc.vector.scalar_tensor_tensor(
                out=factor[:],
                in0=chunk_of(gate_rows, R_COL + a),
                scalar=1.0,
                in1=chunk_of(cand, a),
                op0=ALU.subtract,
                op1=ALU.mult,
            )
            factors[R_COL + a] = factor

        def make_update(a):
            factor = chunks.tile([P, PACK, CHUNK], F32)
            nc.vector.tensor_tensor(
                out=factor[:],
                in0=chunk_of(gate_rows, N_COL + a),
                in1=chunk_of(new_state, a),
                op=ALU.subtract,
            )
            factors[Z_COL + a] = factor

        def product(in0, in1):
            grouped = chunks.tile([P, CHUNK, PACK], BF16, align_bytes=64)
            if in1 is None:
                nc.vector.tensor_scalar(
                    out=column_major_dealt(grouped[:]),
                    in0=token_major_dealt(in0),
                    scalar1=-1.0,
                    scalar2=None,
                    op0=ALU.mult,
                )
            else:
                nc.vector.tensor_tensor(
                    out=column_major_dealt(grouped[:]),
                    in0=token_major_dealt(in0),
                    in1=token_major_dealt(in1),
                    op=ALU.mult,
                )
            return grouped

        def quantise(grouped):
            codes = chunks.tile([P, CHUNK], U32, align_bytes=64)
            scales = chunks.tile([P, CHUNK], U8, align_bytes=64)
            nc.vector.quantize_mx(
                out=codes[:].bitcast(E5M2_X4),
                scales=scales[:],
                in_=grouped[:].rearrange("p w t -> p (w t)"),
            )
            return codes, scales

        def multiply(codes, scales):
            filled = []
            for j in range(TILES):
                m_cols = slice(j * M_TILE, (j + 1) * M_TILE)
                for first in range(0, H, N_TILE):
                    n_cols = slice(first, first + N_TILE)
                    acc = banks.tile([M_TILE, N_TILE], F32)
                    nc.tensor.matmul_mx(
                        out=acc[:],
                        lhsT=codes[:, m_cols].bitcast(E5M2_X4),
                        lhsT_scale=scales[:, m_cols],
                        rhs=state_codes[:, n_cols].bitcast(E4M3_X4),
                        rhs_scale=state_scales[:, n_cols],
                        start=True,
                        stop=True,
                    )
                    filled.append((acc, j, n_cols))
            return filled

        def rows_of_chunk(first_row):
            return out[first_row : first_row + CHUNK, :].rearrange("(p j) n -> p j n", j=TILES)

        products = (
            [(minus_dn[a][:], False, N_COL + a) for a in starts]
            + [(minus_dn[a][:], True, R_COL + a) for a in starts]
            + [(chunk_of(gate_rows, Z_COL + a), True, Z_COL + a) for a in starts]
        )
        for a in starts[:3]:
            make_minus_dn(early, a)
        for a in starts[:2]:
            make_minus_dn(late, a)
        preparations = (
            [
                [lambda: make_minus_dn(early, starts[3])],
                [lambda: make_minus_dn(late, starts[2]), lambda: make_minus_dn(late, starts[3])],
            ]
            + [[lambda a=a: make_reset(a)] for a in starts]
            + [[lambda a=a: make_update(a)] for a in starts]
        )
        count = len(products)
        SHARED = 2
        per_tile = len(halves)
        waiting = []
        for k in range(count):
            in0, with_factor, first_row = products[k]
            grouped = product(in0, factors[first_row][:] if with_factor else None)
            if k < len(preparations):
                for prepare in preparations[k]:
                    prepare()
            codes, scales = quantise(grouped)
            filled = multiply(codes, scales)
            result = rows.tile([M_TILE, TILES, H], F32, align_bytes=4096)
            if k == 0:
                for acc, j, n_cols in filled[:per_tile]:
                    nc.scalar.copy(out=result[:, j, n_cols], in_=acc[:])
                nc.scalar.dma_start(out=rows_of_chunk(first_row)[:, 0, :], in_=result[:, 0, :])
                for acc, j, n_cols in filled[per_tile:]:
                    nc.scalar.copy(out=result[:, j, n_cols], in_=acc[:])
                nc.scalar.dma_start(out=rows_of_chunk(first_row)[:, 1, :], in_=result[:, 1, :])
            elif k < count - SHARED:
                for acc, j, n_cols in filled:
                    nc.scalar.copy(out=result[:, j, n_cols], in_=acc[:])
                nc.scalar.dma_start(out=rows_of_chunk(first_row), in_=result[:])
            else:
                for acc, j, n_cols in filled[:per_tile]:
                    nc.scalar.copy(out=result[:, j, n_cols], in_=acc[:])
                waiting.append((filled[per_tile:], result, first_row))
        for filled, result, first_row in waiting:
            for acc, j, n_cols in filled:
                nc.vector.tensor_copy(out=result[:, j, n_cols], in_=acc[:])
            nc.scalar.dma_start(out=rows_of_chunk(first_row), in_=result[:])
